import numpy as np
import ml_dtypes


def mxq(x, axis, fmt="e4m3"):
    dtype, down = {"e4m3": (ml_dtypes.float8_e4m3fn, 7), "e5m2": (ml_dtypes.float8_e5m2, 14)}[fmt]
    v = np.moveaxis(np.asarray(x, np.float32).astype(ml_dtypes.bfloat16).astype(np.float64), axis, -1)
    blocks = v.reshape(v.shape[:-1] + (-1, 32))
    amax = np.abs(blocks).max(-1, keepdims=True)
    byte = np.maximum(np.where(amax > 0, np.frexp(amax)[1] - 1 + 127, 0) - down, 1)
    scale = np.exp2(byte - 127.0)
    codes = (blocks / scale).astype(np.float32).astype(dtype).astype(np.float64)
    return np.moveaxis((codes * scale).reshape(v.shape), -1, axis)


WIDE = False


def mx_kscale(k):
    if not WIDE:
        return np.ones(k)
    levels = np.array([10, -10, 5, -5, 0])
    a = np.random.permutation(np.resize(levels, k // 512 * 4)).reshape(k // 512, 4)
    idx = np.arange(k)
    return np.exp2(a[idx // 512, idx % 128 // 32])


BF16 = ml_dtypes.bfloat16


def bf(x):
    return np.asarray(x, np.float32).astype(BF16)


def f64(x):
    return np.asarray(x).astype(np.float64)


B, D, H, F, K = 8192, 1024, 256, 1024, 128
EPS_LN = 1e-5


def silu(v):
    return v / (1.0 + np.exp(-v))


def setup_inputs():
    s = mx_kscale(D)
    return {"x": bf(np.random.standard_normal((B, D)) * s),
            "W1": bf(np.random.standard_normal((D, H)) / np.sqrt(D) / s[:, None]),
            "b1": bf(0.2 * np.random.standard_normal(H)),
            "g": bf(1.0 + 0.1 * np.random.standard_normal(H)),
            "beta": bf(0.1 * np.random.standard_normal(H))}


def reference(x, W1, b1, g, beta):
    h = silu((mxq(f64(x), 1, "e4m3") @ mxq(f64(W1), 0, "e4m3")) + f64(b1))
    mu = h.mean(-1, keepdims=True)
    var = ((h - mu) ** 2).mean(-1, keepdims=True)
    return (h - mu) / np.sqrt(var + EPS_LN) * f64(g) + f64(beta)

@@ -1,0 +1,222 @@
+from contextlib import ExitStack
+
+import concourse.mybir as mybir
+from concourse.masks import make_identity
+
+F32 = mybir.dt.float32
+BF16 = mybir.dt.bfloat16
+U32 = mybir.dt.uint32
+U8 = mybir.dt.uint8
+FP8X4 = mybir.dt.float8_e4m3fn_x4
+ACT = mybir.ActivationFunctionType
+ALU = mybir.AluOpType
+
+B, D, H = 8192, 1024, 256
+EPS_LN = 1e-5
+FLOPS = 2 * B * D * H
+
+P = 128
+K_PASS = 512
+PASSES = D // K_PASS
+TILES = 4
+GROUP_ROWS = TILES * P
+GROUPS = B // GROUP_ROWS
+WORDS = D // 2
+BLOCKS = WORDS // P
+
+
+def tile_evidentialhead_pa_t_kernel(tc, x, W1, b1, g, beta, out):
+    nc = tc.nc
+    with ExitStack() as stack:
+        const = stack.enter_context(tc.tile_pool(name="const", bufs=1))
+        x_pool = stack.enter_context(tc.tile_pool(name="x", bufs=4))
+        grouped_pool = stack.enter_context(tc.tile_pool(name="grouped", bufs=3))
+        mx_pool = stack.enter_context(tc.tile_pool(name="mx", bufs=2))
+        work = stack.enter_context(tc.tile_pool(name="work", bufs=3))
+        stats = stack.enter_context(tc.tile_pool(name="stats", bufs=4))
+        xt_psum = stack.enter_context(tc.psum_pool(name="xt_psum", bufs=5))
+        z_psum = stack.enter_context(tc.psum_pool(name="z_psum", bufs=3))
+
+        x_tiles, xt_tiles, grouped_tiles, code_tiles, scale_tiles = {}, {}, {}, {}, {}
+        z_tiles, zb_tiles, h_tiles, t_tiles = {}, {}, {}, {}
+        sum_tiles, negmean_tiles, ssq_tiles, rstd_tiles = {}, {}, {}, {}
+
+        def load_x(i):
+            x_sb = x_pool.tile([P, TILES * D], BF16)
+            rows = x[i * GROUP_ROWS : (i + 1) * GROUP_ROWS, :]
+            nc.sync.dma_start(out=x_sb[:], in_=rows.rearrange("(p n) k -> p (n k)", n=TILES))
+            x_tiles[i] = x_sb
+
+        load_x(0)
+
+        w_raw = const.tile([P, PASSES, 4, H], BF16)
+        nc.sync.dma_start(
+            out=w_raw[:].rearrange("p c (u e) h -> p (c u) (e h)", u=2, e=2),
+            in_=W1.rearrange("(j p e) h -> p j (e h)", j=2 * PASSES, p=P, e=2),
+        )
+        vec_bf = const.tile([P, 3, H], BF16)
+        nc.scalar.dma_start(out=vec_bf[:, 0, :], in_=b1.partition_broadcast(P))
+        nc.scalar.dma_start(out=vec_bf[:, 1, :], in_=g.partition_broadcast(P))
+        nc.scalar.dma_start(out=vec_bf[:, 2, :], in_=beta.partition_broadcast(P))
+
+        ident = const.tile([P, P], F32)
+        make_identity(nc, ident[:])
+        neg_half = const.tile([P, TILES], F32)
+        nc.vector.memset(neg_half[:], -0.5)
+
+        w_grouped = const.tile([P, PASSES, H, 4], BF16, align_bytes=64)
+        nc.vector.tensor_copy(out=w_grouped[:], in_=w_raw[:].rearrange("p c t h -> p c h t"))
+        w_codes = const.tile([P, PASSES * H], U32, align_bytes=64)
+        w_scales = const.tile([P, PASSES * H], U8, align_bytes=64)
+        nc.vector.quantize_mx(
+            out=w_codes[:].bitcast(FP8X4),
+            scales=w_scales[:],
+            in_=w_grouped[:].rearrange("p c h t -> p (c h t)"),
+        )
+        vec = const.tile([P, 3, H], F32)
+        nc.vector.tensor_copy(out=vec[:], in_=vec_bf[:])
+        bias_rows = vec[:, 0:1, :].to_broadcast([P, 2, H])
+        gain = vec[:, 1, :]
+        shift = vec[:, 2, :]
+
+        def transpose_x(i):
+            x_words = x_tiles[i][:].bitcast(F32)
+            for n in range(TILES):
+                xt = xt_psum.tile([P, BLOCKS, P], F32)
+                for j in range(BLOCKS):
+                    first = n * WORDS + j * P
+                    nc.tensor.transpose(xt[:, j, :], x_words[:, first : first + P], ident[:])
+                xt_tiles[(i, n)] = xt
+
+        def copy_xt(i):
+            grouped = grouped_pool.tile([P, PASSES * TILES * P * 4], BF16, align_bytes=64)
+            words = grouped[:].bitcast(F32).rearrange(
+                "p (c n r u) -> p c n r u", c=PASSES, n=TILES, r=P, u=2
+            )
+            for n in range(TILES):
+                nc.scalar.copy(
+                    out=words[:, :, n, :, :],
+                    in_=xt_tiles[(i, n)][:].rearrange("p (c u) r -> p c r u", c=PASSES, u=2),
+                )
+            grouped_tiles[i] = grouped
+
+        def quantise_x(i):
+            codes = mx_pool.tile([P, PASSES * GROUP_ROWS], U32, align_bytes=64)
+            scales = mx_pool.tile([P, PASSES * GROUP_ROWS], U8, align_bytes=64)
+            nc.vector.quantize_mx(
+                out=codes[:].bitcast(FP8X4), scales=scales[:], in_=grouped_tiles[i][:]
+            )
+            code_tiles[i] = codes
+            scale_tiles[i] = scales
+
+        def multiply(i):
+            for half in range(TILES // 2):
+                z = z_psum.tile([P, 2, H], F32)
+                for m in range(2):
+                    n = 2 * half + m
+                    for c in range(PASSES):
+                        x_cols = slice(c * GROUP_ROWS + n * P, c * GROUP_ROWS + (n + 1) * P)
+                        w_cols = slice(c * H, (c + 1) * H)
+                        nc.tensor.matmul_mx(
+                            out=z[:, m, :],
+                            lhsT=code_tiles[i][:, x_cols].bitcast(FP8X4),
+                            lhsT_scale=scale_tiles[i][:, x_cols],
+                            rhs=w_codes[:, w_cols].bitcast(FP8X4),
+                            rhs_scale=w_scales[:, w_cols],
+                            start=(c == 0),
+                            stop=(c == PASSES - 1),
+                        )
+                z_tiles[(i, half)] = z
+
+        def add_bias(i):
+            zb = work.tile([P, TILES, H], F32)
+            for half in range(TILES // 2):
+                nc.vector.tensor_tensor(
+                    out=zb[:, 2 * half : 2 * half + 2, :],
+                    in0=z_tiles[(i, half)][:],
+                    in1=bias_rows,
+                    op=ALU.add,
+                )
+            zb_tiles[i] = zb
+
+        def silu(i):
+            h = work.tile([P, TILES, H], F32)
+            h_sum = stats.tile([P, TILES], F32)
+            for n in range(TILES):
+                nc.scalar.activation(
+                    out=h[:, n, :], in_=zb_tiles[i][:, n, :], func=ACT.Silu,
+                    accum_out=h_sum[:, n : n + 1],
+                )
+            h_tiles[i] = h
+            sum_tiles[i] = h_sum
+
+        def mean(i):
+            negmean = stats.tile([P, TILES], F32)
+            nc.gpsimd.tensor_scalar(
+                out=negmean[:], in0=sum_tiles[i][:], scalar1=-1.0 / H, scalar2=0.0,
+                op0=ALU.mult, op1=ALU.add,
+            )
+            negmean_tiles[i] = negmean
+
+        def variance(i):
+            ssq = stats.tile([P, TILES], F32)
+            for n in range(TILES):
+                squares = work.tile([P, H], F32)
+                nc.scalar.activation(
+                    out=squares[:], in_=h_tiles[i][:, n, :], func=ACT.Square,
+                    bias=negmean_tiles[i][:, n : n + 1], accum_out=ssq[:, n : n + 1],
+                )
+            ssq_tiles[i] = ssq
+
+        def inverse_std(i):
+            var_eps = stats.tile([P, TILES], F32)
+            nc.gpsimd.tensor_scalar(
+                out=var_eps[:], in0=ssq_tiles[i][:], scalar1=1.0 / H, scalar2=EPS_LN,
+                op0=ALU.mult, op1=ALU.add,
+            )
+            rstd = stats.tile([P, TILES], F32)
+            nc.gpsimd.tensor_tensor(out=rstd[:], in0=var_eps[:], in1=neg_half[:], op=ALU.pow)
+            rstd_tiles[i] = rstd
+
+        def centre_and_gain(i):
+            t = work.tile([P, TILES, H], F32)
+            for n in range(TILES):
+                nc.vector.scalar_tensor_tensor(
+                    out=t[:, n, :], in0=h_tiles[i][:, n, :],
+                    scalar=negmean_tiles[i][:, n : n + 1], in1=gain,
+                    op0=ALU.add, op1=ALU.mult,
+                )
+            t_tiles[i] = t
+
+        def scale_shift_store(i):
+            o = work.tile([P, TILES, H], F32)
+            for n in range(TILES):
+                nc.vector.scalar_tensor_tensor(
+                    out=o[:, n, :], in0=t_tiles[i][:, n, :],
+                    scalar=rstd_tiles[i][:, n : n + 1], in1=shift,
+                    op0=ALU.mult, op1=ALU.add,
+                )
+            rows = out[i * GROUP_ROWS : (i + 1) * GROUP_ROWS, :]
+            nc.sync.dma_start(
+                out=rows.rearrange("(p n) h -> p (n h)", n=TILES),
+                in_=o[:].rearrange("p n h -> p (n h)"),
+            )
+
+        def run(stage, i):
+            if 0 <= i < GROUPS:
+                stage(i)
+
+        with tc.manual_schedule():
+            for step in range(-4, GROUPS + 1):
+                run(load_x, step + 5)
+                run(quantise_x, step + 1)
+                run(silu, step)
+                run(multiply, step + 1)
+                run(mean, step)
+                run(copy_xt, step + 2)
+                run(transpose_x, step + 3)
+                run(centre_and_gain, step - 1)
+                run(add_bias, step + 1)
+                run(variance, step)
+                run(inverse_std, step)
+                run(scale_shift_store, step - 1)

@@ -39,7 +39,7 @@ def tile_evidentialhead_pa_t_kernel(tc, x, W1, b1, g, beta, out):
 
         x_tiles, xt_tiles, grouped_tiles, code_tiles, scale_tiles = {}, {}, {}, {}, {}
         z_tiles, zb_tiles, h_tiles, t_tiles = {}, {}, {}, {}
-        sum_tiles, negmean_tiles, ssq_tiles, rstd_tiles = {}, {}, {}, {}
+        sum_tiles, negmean_tiles, var_eps_tiles, rstd_tiles = {}, {}, {}, {}
 
         def load_x(i):
             x_sb = x_pool.tile([P, TILES * D], BF16)
@@ -150,15 +150,10 @@ def tile_evidentialhead_pa_t_kernel(tc, x, W1, b1, g, beta, out):
             h_tiles[i] = h
             sum_tiles[i] = h_sum
 
-        def mean(i):
-            negmean = stats.tile([P, TILES], F32)
-            nc.gpsimd.tensor_scalar(
-                out=negmean[:], in0=sum_tiles[i][:], scalar1=-1.0 / H, scalar2=0.0,
-                op0=ALU.mult, op1=ALU.add,
-            )
-            negmean_tiles[i] = negmean
-
         def variance(i):
+            negmean = stats.tile([P, TILES], F32)
+            nc.scalar.mul(out=negmean[:], in_=sum_tiles[i][:], mul=-1.0 / H)
+            negmean_tiles[i] = negmean
             ssq = stats.tile([P, TILES], F32)
             for n in range(TILES):
                 squares = work.tile([P, H], F32)
@@ -166,16 +161,17 @@ def tile_evidentialhead_pa_t_kernel(tc, x, W1, b1, g, beta, out):
                     out=squares[:], in_=h_tiles[i][:, n, :], func=ACT.Square,
                     bias=negmean_tiles[i][:, n : n + 1], accum_out=ssq[:, n : n + 1],
                 )
-            ssq_tiles[i] = ssq
+            var_eps = stats.tile([P, TILES], F32)
+            nc.scalar.activation(
+                out=var_eps[:], in_=ssq[:], func=ACT.Copy, scale=1.0 / H, bias=EPS_LN
+            )
+            var_eps_tiles[i] = var_eps
 
         def inverse_std(i):
-            var_eps = stats.tile([P, TILES], F32)
-            nc.gpsimd.tensor_scalar(
-                out=var_eps[:], in0=ssq_tiles[i][:], scalar1=1.0 / H, scalar2=EPS_LN,
-                op0=ALU.mult, op1=ALU.add,
-            )
             rstd = stats.tile([P, TILES], F32)
-            nc.gpsimd.tensor_tensor(out=rstd[:], in0=var_eps[:], in1=neg_half[:], op=ALU.pow)
+            nc.gpsimd.tensor_tensor(
+                out=rstd[:], in0=var_eps_tiles[i][:], in1=neg_half[:], op=ALU.pow
+            )
             rstd_tiles[i] = rstd
 
         def centre_and_gain(i):
@@ -207,16 +203,15 @@ def tile_evidentialhead_pa_t_kernel(tc, x, W1, b1, g, beta, out):
                 stage(i)
 
         with tc.manual_schedule():
-            for step in range(-4, GROUPS + 1):
+            for step in range(-4, GROUPS + 2):
                 run(load_x, step + 5)
                 run(quantise_x, step + 1)
-                run(silu, step)
-                run(multiply, step + 1)
-                run(mean, step)
                 run(copy_xt, step + 2)
                 run(transpose_x, step + 3)
-                run(centre_and_gain, step - 1)
-                run(add_bias, step + 1)
+                run(add_bias, step)
+                run(multiply, step + 1)
+                run(silu, step)
                 run(variance, step)
                 run(inverse_std, step)
-                run(scale_shift_store, step - 1)
+                run(centre_and_gain, step - 1)
+                run(scale_shift_store, step - 2)

@@ -23,6 +23,7 @@ GROUP_ROWS = TILES * P
 GROUPS = B // GROUP_ROWS
 WORDS = D // 2
 BLOCKS = WORDS // P
+SCALAR_COPIES = 3
 
 
 def tile_evidentialhead_pa_t_kernel(tc, x, W1, b1, g, beta, out):
@@ -94,10 +95,11 @@ def tile_evidentialhead_pa_t_kernel(tc, x, W1, b1, g, beta, out):
                 "p (c n r u) -> p c n r u", c=PASSES, n=TILES, r=P, u=2
             )
             for n in range(TILES):
-                nc.scalar.copy(
-                    out=words[:, :, n, :, :],
-                    in_=xt_tiles[(i, n)][:].rearrange("p (c u) r -> p c r u", c=PASSES, u=2),
-                )
+                planes = xt_tiles[(i, n)][:].rearrange("p (c u) r -> p c r u", c=PASSES, u=2)
+                if n < SCALAR_COPIES:
+                    nc.scalar.copy(out=words[:, :, n, :, :], in_=planes)
+                else:
+                    nc.vector.tensor_copy(out=words[:, :, n, :, :], in_=planes)
             grouped_tiles[i] = grouped
 
         def quantise_x(i):

@@ -40,7 +40,7 @@ def tile_evidentialhead_pa_t_kernel(tc, x, W1, b1, g, beta, out):
 
         x_tiles, xt_tiles, grouped_tiles, code_tiles, scale_tiles = {}, {}, {}, {}, {}
         z_tiles, zb_tiles, h_tiles, t_tiles = {}, {}, {}, {}
-        sum_tiles, negmean_tiles, var_eps_tiles, rstd_tiles = {}, {}, {}, {}
+        sum_tiles, negmean_tiles, ssq_tiles, rstd_tiles = {}, {}, {}, {}
 
         def load_x(i):
             x_sb = x_pool.tile([P, TILES * D], BF16)
@@ -55,10 +55,13 @@ def tile_evidentialhead_pa_t_kernel(tc, x, W1, b1, g, beta, out):
             out=w_raw[:].rearrange("p c (u e) h -> p (c u) (e h)", u=2, e=2),
             in_=W1.rearrange("(j p e) h -> p j (e h)", j=2 * PASSES, p=P, e=2),
         )
-        vec_bf = const.tile([P, 3, H], BF16)
-        nc.scalar.dma_start(out=vec_bf[:, 0, :], in_=b1.partition_broadcast(P))
-        nc.scalar.dma_start(out=vec_bf[:, 1, :], in_=g.partition_broadcast(P))
-        nc.scalar.dma_start(out=vec_bf[:, 2, :], in_=beta.partition_broadcast(P))
+        vec_rows = const.tile([P, 3, H], BF16)
+        nc.vector.memset(vec_rows[:], 0.0)
+        nc.scalar.dma_start(out=vec_rows[0:1, 0, :], in_=b1.rearrange("(o h) -> o h", o=1))
+        nc.scalar.dma_start(out=vec_rows[0:1, 1, :], in_=g.rearrange("(o h) -> o h", o=1))
+        nc.scalar.dma_start(out=vec_rows[0:1, 2, :], in_=beta.rearrange("(o h) -> o h", o=1))
+        ones = const.tile([P, P], BF16)
+        nc.vector.memset(ones[:], 1.0)
 
         ident = const.tile([P, P], F32)
         make_identity(nc, ident[:])
@@ -75,7 +78,14 @@ def tile_evidentialhead_pa_t_kernel(tc, x, W1, b1, g, beta, out):
             in_=w_grouped[:].rearrange("p c h t -> p (c h t)"),
         )
         vec = const.tile([P, 3, H], F32)
-        nc.vector.tensor_copy(out=vec[:], in_=vec_bf[:])
+        for first in (0, 2):
+            count = min(2, 3 - first)
+            spread = z_psum.tile([P, 2, H], F32, tag="z")
+            nc.tensor.matmul(
+                out=spread[:, 0:count, :], lhsT=ones[:], rhs=vec_rows[:, first : first + count, :],
+                start=True, stop=True,
+            )
+            nc.vector.tensor_copy(out=vec[:, first : first + count, :], in_=spread[:, 0:count, :])
         bias_rows = vec[:, 0:1, :].to_broadcast([P, 2, H])
         gain = vec[:, 1, :]
         shift = vec[:, 2, :]
@@ -113,7 +123,7 @@ def tile_evidentialhead_pa_t_kernel(tc, x, W1, b1, g, beta, out):
 
         def multiply(i):
             for half in range(TILES // 2):
-                z = z_psum.tile([P, 2, H], F32)
+                z = z_psum.tile([P, 2, H], F32, tag="z")
                 for m in range(2):
                     n = 2 * half + m
                     for c in range(PASSES):
@@ -153,27 +163,29 @@ def tile_evidentialhead_pa_t_kernel(tc, x, W1, b1, g, beta, out):
             sum_tiles[i] = h_sum
 
         def variance(i):
-            negmean = stats.tile([P, TILES], F32)
-            nc.scalar.mul(out=negmean[:], in_=sum_tiles[i][:], mul=-1.0 / H)
-            negmean_tiles[i] = negmean
             ssq = stats.tile([P, TILES], F32)
             for n in range(TILES):
                 squares = work.tile([P, H], F32)
                 nc.scalar.activation(
                     out=squares[:], in_=h_tiles[i][:, n, :], func=ACT.Square,
-                    bias=negmean_tiles[i][:, n : n + 1], accum_out=ssq[:, n : n + 1],
+                    scale=-1.0 * H, bias=sum_tiles[i][:, n : n + 1], accum_out=ssq[:, n : n + 1],
                 )
-            var_eps = stats.tile([P, TILES], F32)
-            nc.scalar.activation(
-                out=var_eps[:], in_=ssq[:], func=ACT.Copy, scale=1.0 / H, bias=EPS_LN
-            )
-            var_eps_tiles[i] = var_eps
+            ssq_tiles[i] = ssq
 
-        def inverse_std(i):
-            rstd = stats.tile([P, TILES], F32)
-            nc.gpsimd.tensor_tensor(
-                out=rstd[:], in0=var_eps_tiles[i][:], in1=neg_half[:], op=ALU.pow
+        def small_statistics(i):
+            negmean = stats.tile([P, TILES], F32)
+            nc.gpsimd.tensor_scalar(
+                out=negmean[:], in0=sum_tiles[i][:], scalar1=-1.0 / H, scalar2=0.0,
+                op0=ALU.mult, op1=ALU.add,
             )
+            negmean_tiles[i] = negmean
+            var_eps = stats.tile([P, TILES], F32)
+            nc.gpsimd.tensor_scalar(
+                out=var_eps[:], in0=ssq_tiles[i][:], scalar1=1.0 / (H * H * H), scalar2=EPS_LN,
+                op0=ALU.mult, op1=ALU.add,
+            )
+            rstd = stats.tile([P, TILES], F32)
+            nc.gpsimd.tensor_tensor(out=rstd[:], in0=var_eps[:], in1=neg_half[:], op=ALU.pow)
             rstd_tiles[i] = rstd
 
         def centre_and_gain(i):
@@ -188,17 +200,17 @@ def tile_evidentialhead_pa_t_kernel(tc, x, W1, b1, g, beta, out):
 
         def scale_shift_store(i):
             o = work.tile([P, TILES, H], F32)
+            rows = out[i * GROUP_ROWS : (i + 1) * GROUP_ROWS, :].rearrange(
+                "(p n) h -> p n h", n=TILES
+            )
             for n in range(TILES):
                 nc.vector.scalar_tensor_tensor(
                     out=o[:, n, :], in0=t_tiles[i][:, n, :],
                     scalar=rstd_tiles[i][:, n : n + 1], in1=shift,
                     op0=ALU.mult, op1=ALU.add,
                 )
-            rows = out[i * GROUP_ROWS : (i + 1) * GROUP_ROWS, :]
-            nc.sync.dma_start(
-                out=rows.rearrange("(p n) h -> p (n h)", n=TILES),
-                in_=o[:].rearrange("p n h -> p (n h)"),
-            )
+                if n % 2 == 1:
+                    nc.sync.dma_start(out=rows[:, n - 1 : n + 1, :], in_=o[:, n - 1 : n + 1, :])
 
         def run(stage, i):
             if 0 <= i < GROUPS:
@@ -214,6 +226,6 @@ def tile_evidentialhead_pa_t_kernel(tc, x, W1, b1, g, beta, out):
                 run(multiply, step + 1)
                 run(silu, step)
                 run(variance, step)
-                run(inverse_std, step)
+                run(small_statistics, step)
                 run(centre_and_gain, step - 1)
                 run(scale_shift_store, step - 2)

@@ -23,6 +23,7 @@ GROUP_ROWS = TILES * P
 GROUPS = B // GROUP_ROWS
 WORDS = D // 2
 BLOCKS = WORDS // P
+LOADS_AHEAD = 5
 SCALAR_COPIES = 3
 
 
@@ -42,19 +43,25 @@ def tile_evidentialhead_pa_t_kernel(tc, x, W1, b1, g, beta, out):
         z_tiles, zb_tiles, h_tiles, t_tiles = {}, {}, {}, {}
         sum_tiles, negmean_tiles, ssq_tiles, rstd_tiles = {}, {}, {}, {}
 
-        def load_x(i):
-            x_sb = x_pool.tile([P, TILES * D], BF16)
-            rows = x[i * GROUP_ROWS : (i + 1) * GROUP_ROWS, :]
-            nc.sync.dma_start(out=x_sb[:], in_=rows.rearrange("(p n) k -> p (n k)", n=TILES))
+        def load_x(i, pieces=1):
+            x_sb = x_pool.tile([P, TILES, D], BF16)
+            rows = x[i * GROUP_ROWS : (i + 1) * GROUP_ROWS, :].rearrange("(p n) k -> p n k", n=TILES)
+            count = TILES // pieces
+            for first in range(0, TILES, count):
+                nc.sync.dma_start(
+                    out=x_sb[:, first : first + count, :], in_=rows[:, first : first + count, :]
+                )
             x_tiles[i] = x_sb
 
-        load_x(0)
+        load_x(0, pieces=TILES)
 
         w_raw = const.tile([P, PASSES, 4, H], BF16)
         nc.sync.dma_start(
             out=w_raw[:].rearrange("p c (u e) h -> p (c u) (e h)", u=2, e=2),
             in_=W1.rearrange("(j p e) h -> p j (e h)", j=2 * PASSES, p=P, e=2),
         )
+        for i in range(1, LOADS_AHEAD - 3):
+            load_x(i)
         vec_rows = const.tile([P, 3, H], BF16)
         nc.vector.memset(vec_rows[:], 0.0)
         nc.scalar.dma_start(out=vec_rows[0:1, 0, :], in_=b1.rearrange("(o h) -> o h", o=1))
@@ -78,25 +85,28 @@ def tile_evidentialhead_pa_t_kernel(tc, x, W1, b1, g, beta, out):
             in_=w_grouped[:].rearrange("p c h t -> p (c h t)"),
         )
         vec = const.tile([P, 3, H], F32)
-        for first in (0, 2):
-            count = min(2, 3 - first)
-            spread = z_psum.tile([P, 2, H], F32, tag="z")
-            nc.tensor.matmul(
-                out=spread[:, 0:count, :], lhsT=ones[:], rhs=vec_rows[:, first : first + count, :],
-                start=True, stop=True,
-            )
-            nc.vector.tensor_copy(out=vec[:, first : first + count, :], in_=spread[:, 0:count, :])
         bias_rows = vec[:, 0:1, :].to_broadcast([P, 2, H])
         gain = vec[:, 1, :]
         shift = vec[:, 2, :]
+
+        def spread_vectors():
+            for first in (0, 2):
+                count = min(2, 3 - first)
+                spread = z_psum.tile([P, 2, H], F32, tag="z")
+                nc.tensor.matmul(
+                    out=spread[:, 0:count, :], lhsT=ones[:],
+                    rhs=vec_rows[:, first : first + count, :], start=True, stop=True,
+                )
+                nc.vector.tensor_copy(
+                    out=vec[:, first : first + count, :], in_=spread[:, 0:count, :]
+                )
 
         def transpose_x(i):
             x_words = x_tiles[i][:].bitcast(F32)
             for n in range(TILES):
                 xt = xt_psum.tile([P, BLOCKS, P], F32)
                 for j in range(BLOCKS):
-                    first = n * WORDS + j * P
-                    nc.tensor.transpose(xt[:, j, :], x_words[:, first : first + P], ident[:])
+                    nc.tensor.transpose(xt[:, j, :], x_words[:, n, j * P : (j + 1) * P], ident[:])
                 xt_tiles[(i, n)] = xt
 
         def copy_xt(i):
@@ -217,11 +227,13 @@ def tile_evidentialhead_pa_t_kernel(tc, x, W1, b1, g, beta, out):
                 stage(i)
 
         with tc.manual_schedule():
-            for step in range(-4, GROUPS + 2):
-                run(load_x, step + 5)
+            for step in range(-3, GROUPS + 2):
+                run(load_x, step + LOADS_AHEAD)
                 run(quantise_x, step + 1)
                 run(copy_xt, step + 2)
                 run(transpose_x, step + 3)
+                if step == -1:
+                    spread_vectors()
                 run(add_bias, step)
                 run(multiply, step + 1)
                 run(silu, step)

@@ -18,20 +18,20 @@ FLOPS = 2 * B * D * H
 P = 128
 K_PASS = 512
 PASSES = D // K_PASS
-TILES = 4
+TILES = 2
 GROUP_ROWS = TILES * P
 GROUPS = B // GROUP_ROWS
 WORDS = D // 2
 BLOCKS = WORDS // P
-LOADS_AHEAD = 5
-SCALAR_COPIES = 3
+LOADS_AHEAD = 7
+VECTOR_COPIES_EVERY = 4
 
 
 def tile_evidentialhead_pa_t_kernel(tc, x, W1, b1, g, beta, out):
     nc = tc.nc
     with ExitStack() as stack:
         const = stack.enter_context(tc.tile_pool(name="const", bufs=1))
-        x_pool = stack.enter_context(tc.tile_pool(name="x", bufs=4))
+        x_pool = stack.enter_context(tc.tile_pool(name="x", bufs=6))
         grouped_pool = stack.enter_context(tc.tile_pool(name="grouped", bufs=3))
         mx_pool = stack.enter_context(tc.tile_pool(name="mx", bufs=2))
         work = stack.enter_context(tc.tile_pool(name="work", bufs=3))
@@ -116,10 +116,10 @@ def tile_evidentialhead_pa_t_kernel(tc, x, W1, b1, g, beta, out):
             )
             for n in range(TILES):
                 planes = xt_tiles[(i, n)][:].rearrange("p (c u) r -> p c r u", c=PASSES, u=2)
-                if n < SCALAR_COPIES:
-                    nc.scalar.copy(out=words[:, :, n, :, :], in_=planes)
-                else:
+                if (i * TILES + n) % VECTOR_COPIES_EVERY == VECTOR_COPIES_EVERY - 1:
                     nc.vector.tensor_copy(out=words[:, :, n, :, :], in_=planes)
+                else:
+                    nc.scalar.copy(out=words[:, :, n, :, :], in_=planes)
             grouped_tiles[i] = grouped
 
         def quantise_x(i):

@@ -18,20 +18,20 @@ FLOPS = 2 * B * D * H
 P = 128
 K_PASS = 512
 PASSES = D // K_PASS
-TILES = 2
+TILES = 4
 GROUP_ROWS = TILES * P
 GROUPS = B // GROUP_ROWS
 WORDS = D // 2
 BLOCKS = WORDS // P
-LOADS_AHEAD = 7
-VECTOR_COPIES_EVERY = 4
+LOADS_AHEAD = 5
+SCALAR_COPIES = 3
 
 
 def tile_evidentialhead_pa_t_kernel(tc, x, W1, b1, g, beta, out):
     nc = tc.nc
     with ExitStack() as stack:
         const = stack.enter_context(tc.tile_pool(name="const", bufs=1))
-        x_pool = stack.enter_context(tc.tile_pool(name="x", bufs=6))
+        x_pool = stack.enter_context(tc.tile_pool(name="x", bufs=4))
         grouped_pool = stack.enter_context(tc.tile_pool(name="grouped", bufs=3))
         mx_pool = stack.enter_context(tc.tile_pool(name="mx", bufs=2))
         work = stack.enter_context(tc.tile_pool(name="work", bufs=3))
@@ -116,10 +116,10 @@ def tile_evidentialhead_pa_t_kernel(tc, x, W1, b1, g, beta, out):
             )
             for n in range(TILES):
                 planes = xt_tiles[(i, n)][:].rearrange("p (c u) r -> p c r u", c=PASSES, u=2)
-                if (i * TILES + n) % VECTOR_COPIES_EVERY == VECTOR_COPIES_EVERY - 1:
-                    nc.vector.tensor_copy(out=words[:, :, n, :, :], in_=planes)
-                else:
+                if n < SCALAR_COPIES:
                     nc.scalar.copy(out=words[:, :, n, :, :], in_=planes)
+                else:
+                    nc.vector.tensor_copy(out=words[:, :, n, :, :], in_=planes)
             grouped_tiles[i] = grouped
 
         def quantise_x(i):
@@ -184,13 +184,12 @@ def tile_evidentialhead_pa_t_kernel(tc, x, W1, b1, g, beta, out):
 
         def small_statistics(i):
             negmean = stats.tile([P, TILES], F32)
-            nc.gpsimd.tensor_scalar(
-                out=negmean[:], in0=sum_tiles[i][:], scalar1=-1.0 / H, scalar2=0.0,
-                op0=ALU.mult, op1=ALU.add,
+            nc.vector.tensor_scalar(
+                out=negmean[:], in0=sum_tiles[i][:], scalar1=-1.0 / H, scalar2=None, op0=ALU.mult
             )
             negmean_tiles[i] = negmean
             var_eps = stats.tile([P, TILES], F32)
-            nc.gpsimd.tensor_scalar(
+            nc.vector.tensor_scalar(
                 out=var_eps[:], in0=ssq_tiles[i][:], scalar1=1.0 / (H * H * H), scalar2=EPS_LN,
                 op0=ALU.mult, op1=ALU.add,
             )
@@ -230,6 +229,7 @@ def tile_evidentialhead_pa_t_kernel(tc, x, W1, b1, g, beta, out):
             for step in range(-3, GROUPS + 2):
                 run(load_x, step + LOADS_AHEAD)
                 run(quantise_x, step + 1)
+                run(small_statistics, step - 1)
                 run(copy_xt, step + 2)
                 run(transpose_x, step + 3)
                 if step == -1:
@@ -238,6 +238,5 @@ def tile_evidentialhead_pa_t_kernel(tc, x, W1, b1, g, beta, out):
                 run(multiply, step + 1)
                 run(silu, step)
                 run(variance, step)
-                run(small_statistics, step)
                 run(centre_and_gain, step - 1)
                 run(scale_shift_store, step - 2)

from contextlib import ExitStack

import concourse.mybir as mybir
from concourse.masks import make_identity

F32 = mybir.dt.float32
BF16 = mybir.dt.bfloat16
U32 = mybir.dt.uint32
U8 = mybir.dt.uint8
FP8X4 = mybir.dt.float8_e4m3fn_x4
ACT = mybir.ActivationFunctionType
ALU = mybir.AluOpType

B, D, H = 8192, 1024, 256
EPS_LN = 1e-5
FLOPS = 2 * B * D * H

P = 128
K_PASS = 512
PASSES = D // K_PASS
TILES = 4
GROUP_ROWS = TILES * P
GROUPS = B // GROUP_ROWS
WORDS = D // 2
BLOCKS = WORDS // P
LOADS_AHEAD = 5
SCALAR_COPIES = 3


def tile_evidentialhead_pa_t_kernel(tc, x, W1, b1, g, beta, out):
    nc = tc.nc
    with ExitStack() as stack:
        const = stack.enter_context(tc.tile_pool(name="const", bufs=1))
        x_pool = stack.enter_context(tc.tile_pool(name="x", bufs=4))
        grouped_pool = stack.enter_context(tc.tile_pool(name="grouped", bufs=3))
        mx_pool = stack.enter_context(tc.tile_pool(name="mx", bufs=2))
        work = stack.enter_context(tc.tile_pool(name="work", bufs=3))
        stats = stack.enter_context(tc.tile_pool(name="stats", bufs=4))
        xt_psum = stack.enter_context(tc.psum_pool(name="xt_psum", bufs=5))
        z_psum = stack.enter_context(tc.psum_pool(name="z_psum", bufs=3))

        x_tiles, xt_tiles, grouped_tiles, code_tiles, scale_tiles = {}, {}, {}, {}, {}
        z_tiles, zb_tiles, h_tiles, t_tiles = {}, {}, {}, {}
        sum_tiles, negmean_tiles, ssq_tiles, rstd_tiles = {}, {}, {}, {}

        def load_x(i, pieces=1):
            x_sb = x_pool.tile([P, TILES, D], BF16)
            rows = x[i * GROUP_ROWS : (i + 1) * GROUP_ROWS, :].rearrange("(p n) k -> p n k", n=TILES)
            count = TILES // pieces
            for first in range(0, TILES, count):
                nc.sync.dma_start(
                    out=x_sb[:, first : first + count, :], in_=rows[:, first : first + count, :]
                )
            x_tiles[i] = x_sb

        load_x(0, pieces=TILES)

        w_raw = const.tile([P, PASSES, 4, H], BF16)
        nc.sync.dma_start(
            out=w_raw[:].rearrange("p c (u e) h -> p (c u) (e h)", u=2, e=2),
            in_=W1.rearrange("(j p e) h -> p j (e h)", j=2 * PASSES, p=P, e=2),
        )
        for i in range(1, LOADS_AHEAD - 3):
            load_x(i)
        vec_rows = const.tile([P, 3, H], BF16)
        nc.vector.memset(vec_rows[:], 0.0)
        nc.scalar.dma_start(out=vec_rows[0:1, 0, :], in_=b1.rearrange("(o h) -> o h", o=1))
        nc.scalar.dma_start(out=vec_rows[0:1, 1, :], in_=g.rearrange("(o h) -> o h", o=1))
        nc.scalar.dma_start(out=vec_rows[0:1, 2, :], in_=beta.rearrange("(o h) -> o h", o=1))
        ones = const.tile([P, P], BF16)
        nc.vector.memset(ones[:], 1.0)

        ident = const.tile([P, P], F32)
        make_identity(nc, ident[:])
        neg_half = const.tile([P, TILES], F32)
        nc.vector.memset(neg_half[:], -0.5)

        w_grouped = const.tile([P, PASSES, H, 4], BF16, align_bytes=64)
        nc.vector.tensor_copy(out=w_grouped[:], in_=w_raw[:].rearrange("p c t h -> p c h t"))
        w_codes = const.tile([P, PASSES * H], U32, align_bytes=64)
        w_scales = const.tile([P, PASSES * H], U8, align_bytes=64)
        nc.vector.quantize_mx(
            out=w_codes[:].bitcast(FP8X4),
            scales=w_scales[:],
            in_=w_grouped[:].rearrange("p c h t -> p (c h t)"),
        )
        vec = const.tile([P, 3, H], F32)
        bias_rows = vec[:, 0:1, :].to_broadcast([P, 2, H])
        gain = vec[:, 1, :]
        shift = vec[:, 2, :]

        def spread_vectors():
            for first in (0, 2):
                count = min(2, 3 - first)
                spread = z_psum.tile([P, 2, H], F32, tag="z")
                nc.tensor.matmul(
                    out=spread[:, 0:count, :], lhsT=ones[:],
                    rhs=vec_rows[:, first : first + count, :], start=True, stop=True,
                )
                nc.vector.tensor_copy(
                    out=vec[:, first : first + count, :], in_=spread[:, 0:count, :]
                )

        def transpose_x(i):
            x_words = x_tiles[i][:].bitcast(F32)
            for n in range(TILES):
                xt = xt_psum.tile([P, BLOCKS, P], F32)
                for j in range(BLOCKS):
                    nc.tensor.transpose(xt[:, j, :], x_words[:, n, j * P : (j + 1) * P], ident[:])
                xt_tiles[(i, n)] = xt

        def copy_xt(i):
            grouped = grouped_pool.tile([P, PASSES * TILES * P * 4], BF16, align_bytes=64)
            words = grouped[:].bitcast(F32).rearrange(
                "p (c n r u) -> p c n r u", c=PASSES, n=TILES, r=P, u=2
            )
            for n in range(TILES):
                planes = xt_tiles[(i, n)][:].rearrange("p (c u) r -> p c r u", c=PASSES, u=2)
                if n < SCALAR_COPIES:
                    nc.scalar.copy(out=words[:, :, n, :, :], in_=planes)
                else:
                    nc.vector.tensor_copy(out=words[:, :, n, :, :], in_=planes)
            grouped_tiles[i] = grouped

        def quantise_x(i):
            codes = mx_pool.tile([P, PASSES * GROUP_ROWS], U32, align_bytes=64)
            scales = mx_pool.tile([P, PASSES * GROUP_ROWS], U8, align_bytes=64)
            nc.vector.quantize_mx(
                out=codes[:].bitcast(FP8X4), scales=scales[:], in_=grouped_tiles[i][:]
            )
            code_tiles[i] = codes
            scale_tiles[i] = scales

        def multiply(i):
            for half in range(TILES // 2):
                z = z_psum.tile([P, 2, H], F32, tag="z")
                for m in range(2):
                    n = 2 * half + m
                    for c in range(PASSES):
                        x_cols = slice(c * GROUP_ROWS + n * P, c * GROUP_ROWS + (n + 1) * P)
                        w_cols = slice(c * H, (c + 1) * H)
                        nc.tensor.matmul_mx(
                            out=z[:, m, :],
                            lhsT=code_tiles[i][:, x_cols].bitcast(FP8X4),
                            lhsT_scale=scale_tiles[i][:, x_cols],
                            rhs=w_codes[:, w_cols].bitcast(FP8X4),
                            rhs_scale=w_scales[:, w_cols],
                            start=(c == 0),
                            stop=(c == PASSES - 1),
                        )
                z_tiles[(i, half)] = z

        def add_bias(i):
            zb = work.tile([P, TILES, H], F32)
            for half in range(TILES // 2):
                nc.vector.tensor_tensor(
                    out=zb[:, 2 * half : 2 * half + 2, :],
                    in0=z_tiles[(i, half)][:],
                    in1=bias_rows,
                    op=ALU.add,
                )
            zb_tiles[i] = zb

        def silu(i):
            h = work.tile([P, TILES, H], F32)
            h_sum = stats.tile([P, TILES], F32)
            for n in range(TILES):
                nc.scalar.activation(
                    out=h[:, n, :], in_=zb_tiles[i][:, n, :], func=ACT.Silu,
                    accum_out=h_sum[:, n : n + 1],
                )
            h_tiles[i] = h
            sum_tiles[i] = h_sum

        def variance(i):
            ssq = stats.tile([P, TILES], F32)
            for n in range(TILES):
                squares = work.tile([P, H], F32)
                nc.scalar.activation(
                    out=squares[:], in_=h_tiles[i][:, n, :], func=ACT.Square,
                    scale=-1.0 * H, bias=sum_tiles[i][:, n : n + 1], accum_out=ssq[:, n : n + 1],
                )
            ssq_tiles[i] = ssq

        def small_statistics(i):
            negmean = stats.tile([P, TILES], F32)
            nc.vector.tensor_scalar(
                out=negmean[:], in0=sum_tiles[i][:], scalar1=-1.0 / H, scalar2=None, op0=ALU.mult
            )
            negmean_tiles[i] = negmean
            var_eps = stats.tile([P, TILES], F32)
            nc.vector.tensor_scalar(
                out=var_eps[:], in0=ssq_tiles[i][:], scalar1=1.0 / (H * H * H), scalar2=EPS_LN,
                op0=ALU.mult, op1=ALU.add,
            )
            rstd = stats.tile([P, TILES], F32)
            nc.gpsimd.tensor_tensor(out=rstd[:], in0=var_eps[:], in1=neg_half[:], op=ALU.pow)
            rstd_tiles[i] = rstd

        def centre_and_gain(i):
            t = work.tile([P, TILES, H], F32)
            for n in range(TILES):
                nc.vector.scalar_tensor_tensor(
                    out=t[:, n, :], in0=h_tiles[i][:, n, :],
                    scalar=negmean_tiles[i][:, n : n + 1], in1=gain,
                    op0=ALU.add, op1=ALU.mult,
                )
            t_tiles[i] = t

        def scale_shift_store(i):
            o = work.tile([P, TILES, H], F32)
            rows = out[i * GROUP_ROWS : (i + 1) * GROUP_ROWS, :].rearrange(
                "(p n) h -> p n h", n=TILES
            )
            for n in range(TILES):
                nc.vector.scalar_tensor_tensor(
                    out=o[:, n, :], in0=t_tiles[i][:, n, :],
                    scalar=rstd_tiles[i][:, n : n + 1], in1=shift,
                    op0=ALU.mult, op1=ALU.add,
                )
                if n % 2 == 1:
                    nc.sync.dma_start(out=rows[:, n - 1 : n + 1, :], in_=o[:, n - 1 : n + 1, :])

        def run(stage, i):
            if 0 <= i < GROUPS:
                stage(i)

        with tc.manual_schedule():
            for step in range(-3, GROUPS + 2):
                run(load_x, step + LOADS_AHEAD)
                run(quantise_x, step + 1)
                run(small_statistics, step - 1)
                run(copy_xt, step + 2)
                run(transpose_x, step + 3)
                if step == -1:
                    spread_vectors()
                run(add_bias, step)
                run(multiply, step + 1)
                run(silu, step)
                run(variance, step)
                run(centre_and_gain, step - 1)
                run(scale_shift_store, step - 2)
